import numpy as np
import ml_dtypes


def mxq(x, axis, fmt="e4m3"):
    dtype, down = {"e4m3": (ml_dtypes.float8_e4m3fn, 7), "e5m2": (ml_dtypes.float8_e5m2, 14)}[fmt]
    v = np.moveaxis(np.asarray(x, np.float32).astype(ml_dtypes.bfloat16).astype(np.float64), axis, -1)
    blocks = v.reshape(v.shape[:-1] + (-1, 32))
    amax = np.abs(blocks).max(-1, keepdims=True)
    byte = np.maximum(np.where(amax > 0, np.frexp(amax)[1] - 1 + 127, 0) - down, 1)
    scale = np.exp2(byte - 127.0)
    codes = (blocks / scale).astype(np.float32).astype(dtype).astype(np.float64)
    return np.moveaxis((codes * scale).reshape(v.shape), -1, axis)


WIDE = False


def mx_kscale(k):
    if not WIDE:
        return np.ones(k)
    levels = np.array([10, -10, 5, -5, 0])
    if k % 512:
        return np.exp2(np.random.permutation(np.resize(levels, k // 32))).repeat(32)
    a = np.empty((k // 512, 16))
    for p in range(k // 512):
        a[p, :8] = np.random.permutation(np.resize(levels, 8))
        for g in range(8):
            far = levels[np.abs(levels - a[p, g]) >= 10]
            a[p, g + 8] = far[np.random.randint(len(far))]
    return np.exp2(a.ravel()).repeat(32)


BF16 = ml_dtypes.bfloat16


def bf(x):
    return np.asarray(x, np.float32).astype(BF16)


def f64(x):
    return np.asarray(x).astype(np.float64)


G1, G2, B, DIM, K, N = 16, 16, 16, 2, 512, 512
T = G1 * G2 * B


def sigmoid(v):
    return 1.0 / (1.0 + np.exp(-v))


def setup_inputs():
    s = mx_kscale(T).reshape(G1, G2, B, 1)
    u = mx_kscale(N)
    a = 1.5 / np.sqrt(K)
    r = np.random.standard_normal
    x0 = bf(r((G1, G2, B, K)))
    wf = bf(r((DIM, K, N)) * a)
    uf = bf(r((DIM, DIM, N)) * 0.5)
    biasf = bf(r((DIM, N)) * 0.5)
    wi = bf(r((K, N)) * a)
    ui = bf(r((DIM, N)) * 0.5)
    biasi = bf(r(N) * 0.5)
    wo0 = bf(r((K, N)) * a)
    uo = bf(r((DIM, N)) * 0.5)
    biaso = bf(r(N) * 0.5)
    wc0 = bf(r((K, N)) * a)
    uc = bf(r((DIM, N)) * 0.5)
    biasc = bf(r(N) * 0.5)
    g = bf(r((G1, G2, B, N)) * np.exp2(np.random.randint(-6, 1, (G1, G2, B, 1))) * 16.0 / s * u)
    o = sigmoid(f64(x0) @ f64(wo0) + f64(biaso))
    c = sigmoid(f64(x0) @ f64(wc0) + f64(biasc))
    return {
        "x": bf(f64(x0) * s),
        "wf": wf,
        "uf": uf,
        "biasf": biasf,
        "wi": wi,
        "ui": ui,
        "biasi": biasi,
        "wo": bf(f64(wo0) / u),
        "uo": uo,
        "biaso": biaso,
        "wc": bf(f64(wc0) / u),
        "uc": uc,
        "biasc": biasc,
        "o": np.asarray(o, np.float32),
        "c": np.asarray(c, np.float32),
        "grad_out": g,
    }


def reference(x, wf, uf, biasf, wi, ui, biasi, wo, uo, biaso, wc, uc, biasc, o, c, grad_out):
    g = f64(grad_out).reshape(T, N)
    og = f64(o).reshape(T, N)
    cg = f64(c).reshape(T, N)
    th = np.tanh(cg)
    dzo = g * th * og * (1.0 - og)
    dzc = g * og * (1.0 - th * th) * cg * (1.0 - cg)
    po = mxq(dzo, 1, "e5m2") @ mxq(f64(wo), 1, "e4m3").T
    pc = mxq(dzc, 1, "e5m2") @ mxq(f64(wc), 1, "e4m3").T
    dx = (po + pc).reshape(G1, G2, B, K)
    dwo = mxq(f64(x).reshape(T, K), 0, "e4m3").T @ mxq(dzo, 0, "e5m2")
    return dx, dwo

@@ -1,0 +1,267 @@
+from contextlib import ExitStack
+
+import concourse.mybir as mybir
+from concourse.masks import make_identity
+
+T, N, K = 4096, 512, 512
+FLOPS = 3 * 2 * T * N * K
+BYTES = 2 * T * K + 2 * 2 * K * N + 2 * 4 * T * N + 2 * T * N + 4 * T * K + 4 * K * N
+
+F32 = mybir.dt.float32
+BF16 = mybir.dt.bfloat16
+U32 = mybir.dt.uint32
+U8 = mybir.dt.uint8
+E4M3 = mybir.dt.float8_e4m3fn_x4
+E5M2 = mybir.dt.float8_e5m2_x4
+ACT = mybir.ActivationFunctionType
+ALU = mybir.AluOpType
+
+P = 128
+PACK = 4
+W = 512
+CHUNK = P * PACK
+NCH = T // CHUNK
+
+
+def tile_mdlstm_t_v_kernel(
+    tc, x, wf, uf, biasf, wi, ui, biasi, wo, uo, biaso, wc, uc, biasc, o, c, grad_out, out_0, out_1
+):
+    nc = tc.nc
+
+    def chunks(ap):
+        return ap.flatten_outer_dims().rearrange("(g p j) w -> g p j w", p=P, j=PACK)
+
+    x_v = chunks(x)
+    o_v = chunks(o)
+    c_v = chunks(c)
+    g_v = chunks(grad_out)
+    dx_v = chunks(out_0)
+    dw_v = out_1.rearrange("(a p) n -> p a n", p=P)
+
+    def flat(t):
+        return t[:].rearrange("p j w -> p (j w)")
+
+    with ExitStack() as ctx:
+        sb = ctx.enter_context(tc.tile_pool(name="sb", bufs=1))
+        ps = ctx.enter_context(tc.psum_pool(name="ps", bufs=1))
+
+        ident = sb.tile([P, P], F32, name="ident", tag="ident")
+        make_identity(nc, ident[:])
+        neg_half = sb.tile([P, 1], F32, name="neg_half", tag="neg_half")
+        nc.vector.memset(neg_half[:], -0.5)
+        warm = sb.tile([P, 1], F32, name="warm", tag="warm")
+
+        acc = []
+        for a in range(4):
+            acc_a = ps.tile([P, W], F32, name="acc%d" % a, tag="acc%d" % a)
+            acc.append(acc_a)
+
+        st = {}
+
+        def load(g):
+            for nm, view, dt_, nb in (("c", c_v, F32, 3), ("o", o_v, F32, 3), ("g", g_v, BF16, 3), ("x", x_v, BF16, 2)):
+                t = sb.tile([P, PACK, W], dt_, name=nm, tag=nm, bufs=nb)
+                nc.sync.dma_start(out=t[:], in_=view[g])
+                st[nm, g] = t
+
+        def load_w(nm, w_ap):
+            t = sb.tile([P, PACK, W], BF16, name=nm, tag=nm)
+            nc.sync.dma_start(out=t[:], in_=w_ap.rearrange("(a p) n -> p a n", p=P))
+            st[nm, 0] = t
+
+        def act_th(g):
+            th = sb.tile([P, PACK, W], F32, name="th", tag="th", bufs=2)
+            nc.scalar.activation(out=flat(th), in_=flat(st["c", g]), func=ACT.Tanh)
+            st["th", g] = th
+
+        def act_cq(g):
+            nc.scalar.activation(out=flat(st["c", g]), in_=flat(st["c", g]), func=ACT.Square, bias=neg_half[:, 0:1])
+
+        def act_t2(g):
+            t2 = sb.tile([P, PACK, W], F32, name="t2", tag="t2", bufs=2)
+            nc.scalar.activation(out=flat(t2), in_=flat(st["th", g]), func=ACT.Square)
+            st["t2", g] = t2
+
+        def x_interleave(g):
+            xi = sb.tile([P, W, PACK], BF16, name="xi", tag="xi", bufs=2, align_bytes=64)
+            nc.scalar.copy(out=xi[:], in_=st["x", g][:].rearrange("p j w -> p w j"))
+            st["xi", g] = xi
+
+        def v_p(g):
+            pt = sb.tile([P, PACK, W], F32, name="pt", tag="pt")
+            nc.vector.tensor_tensor(out=flat(pt), in0=flat(st["g", g]), in1=flat(st["o", g]), op=ALU.mult)
+            st["pt", g] = pt
+
+        def v_q(g):
+            nc.vector.scalar_tensor_tensor(
+                out=flat(st["o", g]), in0=flat(st["o", g]), scalar=1.0, in1=flat(st["th", g]),
+                op0=ALU.subtract, op1=ALU.mult,
+            )
+
+        def v_dzo(g):
+            dzo = sb.tile([P, PACK, W], BF16, name="dzo", tag="dzo", bufs=2)
+            nc.vector.scalar_tensor_tensor(
+                out=flat(dzo), in0=flat(st["pt", g]), scalar=-1.0, in1=flat(st["o", g]),
+                op0=ALU.mult, op1=ALU.mult,
+            )
+            st["dzo", g] = dzo
+
+        def v_m(g):
+            nc.vector.scalar_tensor_tensor(
+                out=flat(st["t2", g]), in0=flat(st["t2", g]), scalar=1.0, in1=flat(st["pt", g]),
+                op0=ALU.subtract, op1=ALU.mult,
+            )
+
+        def v_dzc(g):
+            dzc = sb.tile([P, PACK, W], BF16, name="dzc", tag="dzc", bufs=2)
+            nc.vector.scalar_tensor_tensor(
+                out=flat(dzc), in0=flat(st["c", g]), scalar=0.25, in1=flat(st["t2", g]),
+                op0=ALU.subtract, op1=ALU.mult,
+            )
+            st["dzc", g] = dzc
+
+        def v_interleave(g):
+            dzoi = sb.tile([P, W, PACK], BF16, name="dzoi", tag="dzoi", align_bytes=64)
+            nc.vector.tensor_copy(out=dzoi[:], in_=st["dzo", g][:].rearrange("p j w -> p w j"))
+            st["dzoi", g] = dzoi
+
+        def quantize(nm, g, src, fmt):
+            codes = sb.tile([P, W], U32, name=nm + "_c", tag=nm + "_c", align_bytes=64)
+            scales = sb.tile([P, W], U8, name=nm + "_s", tag=nm + "_s", align_bytes=64)
+            nc.vector.quantize_mx(out=codes[:].bitcast(fmt), scales=scales[:], in_=src)
+            st[nm, g] = (codes, scales)
+
+        def bank():
+            b = ps.tile([P, W], F32, name="bank", tag="bank", bufs=4)
+            return b
+
+        def transposes(nm, g):
+            words = flat(st[nm, g]).bitcast(F32)
+            for h in range(2):
+                tp = bank()
+                tv = tp[:].rearrange("m (a u p) -> m a u p", a=2, u=2)
+                for a in range(2):
+                    j = 2 * h + a
+                    for u in range(2):
+                        nc.tensor.transpose(tv[:, a, u, :], words[:, j * 256 + u : (j + 1) * 256 : 2], ident[:])
+                st[nm + "_tp", g, h] = tp
+
+        def copy_out(nm, g, copies):
+            grouped = sb.tile([P, PACK, P, PACK], BF16, name=nm + "_gr", tag=nm + "_gr", align_bytes=64)
+            dst = grouped[:].bitcast(F32)
+            for h in range(2):
+                tp = st[nm + "_tp", g, h]
+                cp = copies[h]
+                cp(out=dst[:, 2 * h : 2 * h + 2, :, :], in_=tp[:].rearrange("m (a u p) -> m a p u", a=2, u=2))
+            st[nm + "_gr", g] = grouped
+
+        def grouped_flat(nm, g):
+            return st[nm + "_gr", g][:].rearrange("m j p t -> m (j p t)")
+
+        def out1(g):
+            xc, xs = st["xq", g]
+            dc, ds = st["tokq", g]
+            for a in range(4):
+                cols = slice(a * P, (a + 1) * P)
+                nc.tensor.matmul_mx(
+                    out=acc[a][:], lhsT=xc[:, cols].bitcast(E4M3), lhsT_scale=xs[:, cols],
+                    rhs=dc[:].bitcast(E5M2), rhs_scale=ds[:], start=(g == 0), stop=(g == NCH - 1),
+                )
+
+        def out0(g, j):
+            op = bank()
+            cols = slice(j * P, (j + 1) * P)
+            for idx, (dn, wn) in enumerate((("oTq", "woq"), ("cTq", "wcq"))):
+                dc, ds = st[dn, g]
+                wcod, wsc = st[wn, 0]
+                nc.tensor.matmul_mx(
+                    out=op[:], lhsT=dc[:, cols].bitcast(E5M2), lhsT_scale=ds[:, cols],
+                    rhs=wcod[:].bitcast(E4M3), rhs_scale=wsc[:], start=(idx == 0), stop=(idx == 1),
+                )
+            st["op", g, j] = op
+
+        def evac(g, j, copy):
+            if j == 0:
+                dxs = sb.tile([P, PACK, W], F32, name="dxs", tag="dxs", bufs=2)
+                st["dxs", g] = dxs
+            copy(out=st["dxs", g][:, j, :], in_=st["op", g, j][:])
+
+        def store(g, h):
+            nc.sync.dma_start(out=dx_v[g][:, 2 * h : 2 * h + 2, :], in_=st["dxs", g][:, 2 * h : 2 * h + 2, :])
+
+        s_copy = nc.scalar.copy
+        v_copy = nc.vector.tensor_copy
+
+        with tc.manual_schedule():
+            nc.scalar.activation(out=warm[:], in_=neg_half[:], func=ACT.Tanh)
+            load(0)
+            load_w("wo", wo)
+            load_w("wc", wc)
+            load(1)
+            act_th(0)
+            act_t2(0)
+            act_cq(0)
+            x_interleave(0)
+
+            for i in range(NCH + 2):
+                cur = i < NCH
+                prev = 1 <= i <= NCH
+                nxt = i + 1 < NCH
+                if i + 2 < NCH:
+                    load(i + 2)
+                if 2 <= i:
+                    evac(i - 2, 2, s_copy)
+                    evac(i - 2, 3, s_copy if cur else v_copy)
+                    store(i - 2, 1)
+                if prev:
+                    out1(i - 1)
+                    transposes("dzc", i - 1)
+                if i == 0:
+                    transposes("wo", 0)
+                    transposes("wc", 0)
+                if cur:
+                    v_p(i)
+                    v_q(i)
+                if nxt:
+                    act_th(i + 1)
+                    act_cq(i + 1)
+                if prev:
+                    copy_out("dzc", i - 1, (s_copy, s_copy if cur else v_copy))
+                    quantize("oTq", i - 1, grouped_flat("dzo", i - 1), E5M2)
+                if i == 0:
+                    copy_out("wo", 0, (v_copy, v_copy))
+                    copy_out("wc", 0, (v_copy, v_copy))
+                if cur:
+                    v_dzo(i)
+                    transposes("dzo", i)
+                if nxt:
+                    act_t2(i + 1)
+                    x_interleave(i + 1)
+                if cur:
+                    v_m(i)
+                if prev:
+                    quantize("cTq", i - 1, grouped_flat("dzc", i - 1), E5M2)
+                if i == 0:
+                    quantize("woq", 0, grouped_flat("wo", 0), E4M3)
+                    quantize("wcq", 0, grouped_flat("wc", 0), E4M3)
+                if cur:
+                    copy_out("dzo", i, (s_copy, s_copy))
+                if prev:
+                    for j in range(PACK):
+                        out0(i - 1, j)
+                if cur:
+                    v_dzc(i)
+                if prev:
+                    evac(i - 1, 0, s_copy)
+                    evac(i - 1, 1, s_copy if cur else v_copy)
+                    store(i - 1, 0)
+                if cur:
+                    v_interleave(i)
+                    quantize("xq", i, st["xi", i][:].rearrange("p w j -> p (w j)"), E4M3)
+                    quantize("tokq", i, st["dzoi", i][:].rearrange("p w j -> p (w j)"), E5M2)
+                if i == NCH:
+                    dws = sb.tile([P, PACK, W], F32, name="dws", tag="dxs", bufs=2)
+                    for a in range(4):
+                        cp_a = s_copy if a % 2 == 0 else v_copy
+                        cp_a(out=dws[:, a, :], in_=acc[a][:])
+                    nc.sync.dma_start(out=dw_v, in_=dws[:])

@@ -22,6 +22,10 @@ W = 512
 CHUNK = P * PACK
 NCH = T // CHUNK
 
+V_SHARE = (512, 256, 192, 192, 192, 192, 192, 128)
+HALVES = ((0, 2), (2, 4))
+SLOTS = ((0, 1), (1, 2), (2, 3), (3, 4))
+
 
 def tile_mdlstm_t_v_kernel(
     tc, x, wf, uf, biasf, wi, ui, biasi, wo, uo, biaso, wc, uc, biasc, o, c, grad_out, out_0, out_1
@@ -38,8 +42,8 @@ def tile_mdlstm_t_v_kernel(
     dx_v = chunks(out_0)
     dw_v = out_1.rearrange("(a p) n -> p a n", p=P)
 
-    def flat(t):
-        return t[:].rearrange("p j w -> p (j w)")
+    def flat(t, js=(0, 4)):
+        return t[:, js[0] : js[1], :].rearrange("p j w -> p (j w)")
 
     with ExitStack() as ctx:
         sb = ctx.enter_context(tc.tile_pool(name="sb", bufs=1))
@@ -47,6 +51,8 @@ def tile_mdlstm_t_v_kernel(
 
         ident = sb.tile([P, P], F32, name="ident", tag="ident")
         make_identity(nc, ident[:])
+        ident_bf = sb.tile([P, P], BF16, name="ident_bf", tag="ident_bf")
+        make_identity(nc, ident_bf[:])
         neg_half = sb.tile([P, 1], F32, name="neg_half", tag="neg_half")
         nc.vector.memset(neg_half[:], -0.5)
         warm = sb.tile([P, 1], F32, name="warm", tag="warm")
@@ -58,105 +64,136 @@ def tile_mdlstm_t_v_kernel(
 
         st = {}
 
-        def load(g):
-            for nm, view, dt_, nb in (("c", c_v, F32, 3), ("o", o_v, F32, 3), ("g", g_v, BF16, 3), ("x", x_v, BF16, 2)):
+        def alloc_in(g):
+            for nm, dt_, nb in (("c", F32, 3), ("o", F32, 3), ("g", BF16, 3), ("x", BF16, 2)):
                 t = sb.tile([P, PACK, W], dt_, name=nm, tag=nm, bufs=nb)
-                nc.sync.dma_start(out=t[:], in_=view[g])
                 st[nm, g] = t
+
+        def load(nm, view, g, js=(0, 4)):
+            nc.sync.dma_start(out=st[nm, g][:, js[0] : js[1], :], in_=view[g][:, js[0] : js[1], :])
+
+        def load_chunk(g):
+            alloc_in(g)
+            load("c", c_v, g)
+            load("x", x_v, g)
+            load("g", g_v, g)
+            load("o", o_v, g)
 
         def load_w(nm, w_ap):
             t = sb.tile([P, PACK, W], BF16, name=nm, tag=nm)
             nc.sync.dma_start(out=t[:], in_=w_ap.rearrange("(a p) n -> p a n", p=P))
             st[nm, 0] = t
 
-        def act_th(g):
+        def alloc_act(g):
             th = sb.tile([P, PACK, W], F32, name="th", tag="th", bufs=2)
-            nc.scalar.activation(out=flat(th), in_=flat(st["c", g]), func=ACT.Tanh)
-            st["th", g] = th
-
-        def act_cq(g):
-            nc.scalar.activation(out=flat(st["c", g]), in_=flat(st["c", g]), func=ACT.Square, bias=neg_half[:, 0:1])
-
-        def act_t2(g):
             t2 = sb.tile([P, PACK, W], F32, name="t2", tag="t2", bufs=2)
-            nc.scalar.activation(out=flat(t2), in_=flat(st["th", g]), func=ACT.Square)
+            st["th", g] = th
             st["t2", g] = t2
 
-        def x_interleave(g):
-            xi = sb.tile([P, W, PACK], BF16, name="xi", tag="xi", bufs=2, align_bytes=64)
-            nc.scalar.copy(out=xi[:], in_=st["x", g][:].rearrange("p j w -> p w j"))
-            st["xi", g] = xi
+        def act_th(g, js=(0, 4)):
+            nc.scalar.activation(out=flat(st["th", g], js), in_=flat(st["c", g], js), func=ACT.Tanh)
 
-        def v_p(g):
+        def act_cq(g, js=(0, 4)):
+            nc.scalar.activation(out=flat(st["c", g], js), in_=flat(st["c", g], js), func=ACT.Square, bias=neg_half[:, 0:1])
+
+        def act_t2(g, js=(0, 4)):
+            nc.scalar.activation(out=flat(st["t2", g], js), in_=flat(st["th", g], js), func=ACT.Square)
+
+        def alloc_v(g):
             pt = sb.tile([P, PACK, W], F32, name="pt", tag="pt")
-            nc.vector.tensor_tensor(out=flat(pt), in0=flat(st["g", g]), in1=flat(st["o", g]), op=ALU.mult)
-            st["pt", g] = pt
-
-        def v_q(g):
-            nc.vector.scalar_tensor_tensor(
-                out=flat(st["o", g]), in0=flat(st["o", g]), scalar=1.0, in1=flat(st["th", g]),
-                op0=ALU.subtract, op1=ALU.mult,
-            )
-
-        def v_dzo(g):
             dzo = sb.tile([P, PACK, W], BF16, name="dzo", tag="dzo", bufs=2)
-            nc.vector.scalar_tensor_tensor(
-                out=flat(dzo), in0=flat(st["pt", g]), scalar=-1.0, in1=flat(st["o", g]),
-                op0=ALU.mult, op1=ALU.mult,
-            )
-            st["dzo", g] = dzo
-
-        def v_m(g):
-            nc.vector.scalar_tensor_tensor(
-                out=flat(st["t2", g]), in0=flat(st["t2", g]), scalar=1.0, in1=flat(st["pt", g]),
-                op0=ALU.subtract, op1=ALU.mult,
-            )
-
-        def v_dzc(g):
             dzc = sb.tile([P, PACK, W], BF16, name="dzc", tag="dzc", bufs=2)
-            nc.vector.scalar_tensor_tensor(
-                out=flat(dzc), in0=flat(st["c", g]), scalar=0.25, in1=flat(st["t2", g]),
-                op0=ALU.subtract, op1=ALU.mult,
-            )
+            dzoi = sb.tile([P, W, PACK], BF16, name="dzoi", tag="dzoi", bufs=2, align_bytes=64)
+            st["pt", g] = pt
+            st["dzo", g] = dzo
             st["dzc", g] = dzc
-
-        def v_interleave(g):
-            dzoi = sb.tile([P, W, PACK], BF16, name="dzoi", tag="dzoi", align_bytes=64)
-            nc.vector.tensor_copy(out=dzoi[:], in_=st["dzo", g][:].rearrange("p j w -> p w j"))
             st["dzoi", g] = dzoi
 
-        def quantize(nm, g, src, fmt):
-            codes = sb.tile([P, W], U32, name=nm + "_c", tag=nm + "_c", align_bytes=64)
-            scales = sb.tile([P, W], U8, name=nm + "_s", tag=nm + "_s", align_bytes=64)
-            nc.vector.quantize_mx(out=codes[:].bitcast(fmt), scales=scales[:], in_=src)
-            st[nm, g] = (codes, scales)
+        def v_p(g, js=(0, 4)):
+            nc.vector.tensor_tensor(out=flat(st["pt", g], js), in0=flat(st["g", g], js), in1=flat(st["o", g], js), op=ALU.mult)
+
+        def v_q(g, js=(0, 4)):
+            nc.vector.scalar_tensor_tensor(
+                out=flat(st["o", g], js), in0=flat(st["o", g], js), scalar=1.0, in1=flat(st["th", g], js),
+                op0=ALU.subtract, op1=ALU.mult,
+            )
+
+        def v_dzo(g, js=(0, 4)):
+            nc.vector.scalar_tensor_tensor(
+                out=flat(st["dzo", g], js), in0=flat(st["pt", g], js), scalar=-1.0, in1=flat(st["o", g], js),
+                op0=ALU.mult, op1=ALU.mult,
+            )
+
+        def v_m(g, js=(0, 4)):
+            nc.vector.scalar_tensor_tensor(
+                out=flat(st["t2", g], js), in0=flat(st["t2", g], js), scalar=1.0, in1=flat(st["pt", g], js),
+                op0=ALU.subtract, op1=ALU.mult,
+            )
+
+        def v_dzc(g, js=(0, 4)):
+            nc.vector.scalar_tensor_tensor(
+                out=flat(st["dzc", g], js), in0=flat(st["c", g], js), scalar=0.25, in1=flat(st["t2", g], js),
+                op0=ALU.subtract, op1=ALU.mult,
+            )
+
+        def interleave(g, copy, w0, w1):
+            if w1 > w0:
+                copy(out=st["dzoi", g][:, w0:w1, :], in_=st["dzo", g][:, :, w0:w1].rearrange("p j w -> p w j"))
+
+        def quantize(nm, g, src, fmt, js=(0, 4)):
+            if js[0] == 0:
+                codes = sb.tile([P, W], U32, name=nm + "_c", tag=nm + "_c", align_bytes=64)
+                scales = sb.tile([P, W], U8, name=nm + "_s", tag=nm + "_s", align_bytes=64)
+                st[nm, g] = (codes, scales)
+            codes, scales = st[nm, g]
+            cols = slice(js[0] * P, js[1] * P)
+            if src.ndim == 4:
+                part = src[:, js[0] : js[1], :, :].rearrange("p a b c -> p (a b c)")
+            else:
+                part = src[:].rearrange("p a b -> p (a b)")
+            nc.vector.quantize_mx(out=codes[:, cols].bitcast(fmt), scales=scales[:, cols], in_=part)
 
         def bank():
             b = ps.tile([P, W], F32, name="bank", tag="bank", bufs=4)
             return b
 
-        def transposes(nm, g):
-            words = flat(st[nm, g]).bitcast(F32)
-            for h in range(2):
-                tp = bank()
-                tv = tp[:].rearrange("m (a u p) -> m a u p", a=2, u=2)
-                for a in range(2):
-                    j = 2 * h + a
-                    for u in range(2):
-                        nc.tensor.transpose(tv[:, a, u, :], words[:, j * 256 + u : (j + 1) * 256 : 2], ident[:])
-                st[nm + "_tp", g, h] = tp
+        def transposes(nm, g, js):
+            n = js[1] - js[0]
+            tp = bank()
+            tv = tp[:, 0 : n * 2 * P].rearrange("m (a u p) -> m a u p", a=n, u=2)
+            for a in range(n):
+                words = flat(st[nm, g], (js[0] + a, js[0] + a + 1)).bitcast(F32)
+                for u in range(2):
+                    nc.tensor.transpose(tv[:, a, u, :], words[:, u : W // 2 : 2], ident[:])
+            st[nm + "_tp", g, js[0]] = tp
 
-        def copy_out(nm, g, copies):
-            grouped = sb.tile([P, PACK, P, PACK], BF16, name=nm + "_gr", tag=nm + "_gr", align_bytes=64)
-            dst = grouped[:].bitcast(F32)
+        def copy_out(nm, g, js, copy):
+            n = js[1] - js[0]
+            if js[0] == 0:
+                grouped = sb.tile([P, PACK, P, PACK], BF16, name=nm + "_gr", tag=nm + "_gr", align_bytes=64)
+                st[nm + "_gr", g] = grouped
+            dst = st[nm + "_gr", g][:].bitcast(F32)
+            tp = st[nm + "_tp", g, js[0]]
+            copy(out=dst[:, js[0] : js[1], :, :], in_=tp[:, 0 : n * 2 * P].rearrange("m (a u p) -> m a p u", a=n, u=2))
+
+        def x_move(g):
             for h in range(2):
-                tp = st[nm + "_tp", g, h]
+                xb = bank()
+                xb_bf = xb[:].bitcast(BF16)
+                for r in range(2):
+                    w0 = (2 * h + r) * P
+                    nc.tensor.matmul(
+                        out=xb_bf[:, r * W : (r + 1) * W], lhsT=ident_bf[:],
+                        rhs=st["x", g][:, :, w0 : w0 + P].rearrange("p j w -> p w j"), start=True, stop=True,
+                    )
+                st["xb", g, h] = xb
+
+        def x_evac(g, copies):
+            xi = sb.tile([P, 2, 2 * W], BF16, name="xi", tag="xi", bufs=2, align_bytes=64)
+            for h in range(2):
                 cp = copies[h]
-                cp(out=dst[:, 2 * h : 2 * h + 2, :, :], in_=tp[:].rearrange("m (a u p) -> m a p u", a=2, u=2))
-            st[nm + "_gr", g] = grouped
-
-        def grouped_flat(nm, g):
-            return st[nm + "_gr", g][:].rearrange("m j p t -> m (j p t)")
+                cp(out=xi[:, h, :], in_=st["xb", g, h][:].bitcast(BF16))
+            st["xi", g] = xi
 
         def out1(g):
             xc, xs = st["xq", g]
@@ -186,82 +223,148 @@ def tile_mdlstm_t_v_kernel(
                 st["dxs", g] = dxs
             copy(out=st["dxs", g][:, j, :], in_=st["op", g, j][:])
 
-        def store(g, h):
-            nc.sync.dma_start(out=dx_v[g][:, 2 * h : 2 * h + 2, :], in_=st["dxs", g][:, 2 * h : 2 * h + 2, :])
+        def store(g, j0, j1):
+            nc.sync.dma_start(out=dx_v[g][:, j0:j1, :], in_=st["dxs", g][:, j0:j1, :])
 
         s_copy = nc.scalar.copy
         v_copy = nc.vector.tensor_copy
 
         with tc.manual_schedule():
             nc.scalar.activation(out=warm[:], in_=neg_half[:], func=ACT.Tanh)
-            load(0)
+            alloc_in(0)
+            for js in SLOTS:
+                load("c", c_v, 0, js)
+                load("g", g_v, 0, js)
+                load("o", o_v, 0, js)
+            alloc_in(1)
+            load("c", c_v, 1)
+            load("x", x_v, 0)
             load_w("wo", wo)
             load_w("wc", wc)
-            load(1)
-            act_th(0)
-            act_t2(0)
-            act_cq(0)
-            x_interleave(0)
+            load("x", x_v, 1)
+            load("g", g_v, 1)
+            load("o", o_v, 1)
+            alloc_act(0)
+            for js in SLOTS:
+                act_th(0, js)
+                act_t2(0, js)
+                act_cq(0, js)
+            x_move(0)
 
-            for i in range(NCH + 2):
-                cur = i < NCH
-                prev = 1 <= i <= NCH
+            for i in range(NCH):
                 nxt = i + 1 < NCH
+                last = i == NCH - 1
                 if i + 2 < NCH:
-                    load(i + 2)
-                if 2 <= i:
-                    evac(i - 2, 2, s_copy)
-                    evac(i - 2, 3, s_copy if cur else v_copy)
-                    store(i - 2, 1)
-                if prev:
-                    out1(i - 1)
-                    transposes("dzc", i - 1)
-                if i == 0:
-                    transposes("wo", 0)
-                    transposes("wc", 0)
-                if cur:
-                    v_p(i)
-                    v_q(i)
+                    load_chunk(i + 2)
+                alloc_v(i)
                 if nxt:
+                    alloc_act(i + 1)
+                if i == 0:
+                    for js in SLOTS:
+                        v_p(0, js)
+                        v_q(0, js)
+                        v_m(0, js)
+                        v_dzo(0, js)
+                        v_dzc(0, js)
+                    act_th(1)
+                    x_evac(0, (s_copy, s_copy))
+                    for nm in ("wo", "wc"):
+                        for js in HALVES:
+                            transposes(nm, 0, js)
+                    act_cq(1)
+                    for nm in ("wo", "wc"):
+                        for js in HALVES:
+                            copy_out(nm, 0, js, s_copy)
+                    x_move(1)
+                    for js in HALVES:
+                        transposes("dzo", 0, js)
+                    x_evac(1, (s_copy, s_copy))
+                    act_t2(1)
+                    interleave(0, v_copy, 0, V_SHARE[0])
+                    quantize("woq", 0, st["wo_gr", 0], E4M3)
+                    quantize("wcq", 0, st["wc_gr", 0], E4M3)
+                    for js in HALVES:
+                        copy_out("dzo", 0, js, s_copy)
+                    interleave(0, s_copy, V_SHARE[0], W)
+                    quantize("xq", 0, st["xi", 0], E4M3)
+                    continue
+                for js in HALVES:
+                    transposes("dzc", i - 1, js)
+                v_p(i)
+                quantize("tokq", i - 1, st["dzoi", i - 1], E5M2)
+                out1(i - 1)
+                for js in HALVES:
+                    copy_out("dzc", i - 1, js, s_copy)
+                if nxt:
+                    x_move(i + 1)
                     act_th(i + 1)
                     act_cq(i + 1)
-                if prev:
-                    copy_out("dzc", i - 1, (s_copy, s_copy if cur else v_copy))
-                    quantize("oTq", i - 1, grouped_flat("dzo", i - 1), E5M2)
-                if i == 0:
-                    copy_out("wo", 0, (v_copy, v_copy))
-                    copy_out("wc", 0, (v_copy, v_copy))
-                if cur:
-                    v_dzo(i)
-                    transposes("dzo", i)
+                    x_evac(i + 1, (s_copy, s_copy))
+                v_q(i)
+                quantize("oTq", i - 1, st["dzo_gr", i - 1], E5M2)
+                quantize("cTq", i - 1, st["dzc_gr", i - 1], E5M2)
+                for j in range(PACK):
+                    out0(i - 1, j)
+                v_dzo(i)
+                evac(i - 1, 0, s_copy)
+                evac(i - 1, 1, s_copy)
+                store(i - 1, 0, 2)
+                for js in HALVES:
+                    transposes("dzo", i, js)
                 if nxt:
                     act_t2(i + 1)
-                    x_interleave(i + 1)
-                if cur:
+                else:
+                    interleave(i, s_copy, V_SHARE[i], W)
+                evac(i - 1, 2, s_copy)
+                evac(i - 1, 3, s_copy)
+                store(i - 1, 2, 4)
+                if not last:
                     v_m(i)
-                if prev:
-                    quantize("cTq", i - 1, grouped_flat("dzc", i - 1), E5M2)
-                if i == 0:
-                    quantize("woq", 0, grouped_flat("wo", 0), E4M3)
-                    quantize("wcq", 0, grouped_flat("wc", 0), E4M3)
-                if cur:
-                    copy_out("dzo", i, (s_copy, s_copy))
-                if prev:
-                    for j in range(PACK):
-                        out0(i - 1, j)
-                if cur:
+                    interleave(i, v_copy, 0, V_SHARE[i])
+                    for js in HALVES:
+                        copy_out("dzo", i, js, s_copy)
+                    interleave(i, s_copy, V_SHARE[i], W)
                     v_dzc(i)
-                if prev:
-                    evac(i - 1, 0, s_copy)
-                    evac(i - 1, 1, s_copy if cur else v_copy)
-                    store(i - 1, 0)
-                if cur:
-                    v_interleave(i)
-                    quantize("xq", i, st["xi", i][:].rearrange("p w j -> p (w j)"), E4M3)
-                    quantize("tokq", i, st["dzoi", i][:].rearrange("p w j -> p (w j)"), E5M2)
-                if i == NCH:
-                    dws = sb.tile([P, PACK, W], F32, name="dws", tag="dxs", bufs=2)
-                    for a in range(4):
-                        cp_a = s_copy if a % 2 == 0 else v_copy
-                        cp_a(out=dws[:, a, :], in_=acc[a][:])
-                    nc.sync.dma_start(out=dw_v, in_=dws[:])
+                    quantize("xq", i, st["xi", i], E4M3)
+                else:
+                    quantize("xq", i, st["xi", i], E4M3)
+                    interleave(i, v_copy, 0, V_SHARE[i])
+                    v_m(i, (0, 2))
+                    quantize("tokq", i, st["dzoi", i], E5M2)
+                    out1(i)
+                    for js in HALVES:
+                        copy_out("dzo", i, js, s_copy)
+                    v_dzc(i, (0, 2))
+                    transposes("dzc", i, (0, 2))
+                    dws = sb.tile([P, PACK, W], F32, name="dws", tag="dws")
+                    s_copy(out=dws[:, 0, :], in_=acc[0][:])
+                    s_copy(out=dws[:, 1, :], in_=acc[1][:])
+                    nc.sync.dma_start(out=dw_v[:, 0:2, :], in_=dws[:, 0:2, :])
+                    v_m(i, (2, 3))
+                    quantize("oTq", i, st["dzo_gr", i], E5M2)
+                    v_dzc(i, (2, 3))
+                    transposes("dzc", i, (2, 3))
+                    copy_out("dzc", i, (0, 2), s_copy)
+                    v_m(i, (3, 4))
+                    quantize("cTq", i, st["dzc_gr", i], E5M2, (0, 2))
+                    out0(i, 0)
+                    out0(i, 1)
+                    v_dzc(i, (3, 4))
+                    transposes("dzc", i, (3, 4))
+                    s_copy(out=dws[:, 2, :], in_=acc[2][:])
+                    copy_out("dzc", i, (2, 3), s_copy)
+                    quantize("cTq", i, st["dzc_gr", i], E5M2, (2, 3))
+                    out0(i, 2)
+                    s_copy(out=dws[:, 3, :], in_=acc[3][:])
+                    nc.sync.dma_start(out=dw_v[:, 2:4, :], in_=dws[:, 2:4, :])
+                    evac(i, 0, v_copy)
+                    store(i, 0, 1)
+                    copy_out("dzc", i, (3, 4), s_copy)
+                    quantize("cTq", i, st["dzc_gr", i], E5M2, (3, 4))
+                    out0(i, 3)
+                    evac(i, 1, s_copy)
+                    store(i, 1, 2)
+                    evac(i, 2, v_copy)
+                    store(i, 2, 3)
+                    evac(i, 3, s_copy)
+                    store(i, 3, 4)

@@ -275,17 +275,16 @@ def tile_mdlstm_t_v_kernel(
                     for nm in ("wo", "wc"):
                         for js in HALVES:
                             copy_out(nm, 0, js, s_copy)
-                    x_move(1)
                     for js in HALVES:
                         transposes("dzo", 0, js)
-                    x_evac(1, (s_copy, s_copy))
+                    x_move(1)
                     act_t2(1)
                     interleave(0, v_copy, 0, V_SHARE[0])
                     quantize("woq", 0, st["wo_gr", 0], E4M3)
                     quantize("wcq", 0, st["wc_gr", 0], E4M3)
+                    interleave(0, s_copy, V_SHARE[0], W)
                     for js in HALVES:
                         copy_out("dzo", 0, js, s_copy)
-                    interleave(0, s_copy, V_SHARE[0], W)
                     quantize("xq", 0, st["xi", 0], E4M3)
                     continue
                 for js in HALVES:
@@ -293,37 +292,45 @@ def tile_mdlstm_t_v_kernel(
                 v_p(i)
                 quantize("tokq", i - 1, st["dzoi", i - 1], E5M2)
                 out1(i - 1)
+                if nxt:
+                    act_th(i + 1)
+                x_evac(i, (s_copy, s_copy))
+                if nxt:
+                    act_cq(i + 1)
                 for js in HALVES:
                     copy_out("dzc", i - 1, js, s_copy)
-                if nxt:
-                    x_move(i + 1)
-                    act_th(i + 1)
-                    act_cq(i + 1)
-                    x_evac(i + 1, (s_copy, s_copy))
                 v_q(i)
                 quantize("oTq", i - 1, st["dzo_gr", i - 1], E5M2)
-                quantize("cTq", i - 1, st["dzc_gr", i - 1], E5M2)
+                if last:
+                    quantize("cTq", i - 1, st["dzc_gr", i - 1], E5M2)
+                    v_dzo(i)
+                else:
+                    v_dzo(i)
+                    quantize("cTq", i - 1, st["dzc_gr", i - 1], E5M2)
                 for j in range(PACK):
                     out0(i - 1, j)
-                v_dzo(i)
+                if nxt:
+                    act_t2(i + 1)
                 evac(i - 1, 0, s_copy)
                 evac(i - 1, 1, s_copy)
                 store(i - 1, 0, 2)
                 for js in HALVES:
                     transposes("dzo", i, js)
-                if nxt:
-                    act_t2(i + 1)
-                else:
+                if last:
                     interleave(i, s_copy, V_SHARE[i], W)
-                evac(i - 1, 2, s_copy)
-                evac(i - 1, 3, s_copy)
-                store(i - 1, 2, 4)
+                    evac(i - 1, 2, s_copy)
+                    evac(i - 1, 3, s_copy)
+                    store(i - 1, 2, 4)
                 if not last:
                     v_m(i)
                     interleave(i, v_copy, 0, V_SHARE[i])
+                    interleave(i, s_copy, V_SHARE[i], W)
+                    evac(i - 1, 2, s_copy)
+                    evac(i - 1, 3, s_copy)
+                    store(i - 1, 2, 4)
+                    x_move(i + 1)
                     for js in HALVES:
                         copy_out("dzo", i, js, s_copy)
-                    interleave(i, s_copy, V_SHARE[i], W)
                     v_dzc(i)
                     quantize("xq", i, st["xi", i], E4M3)
                 else:

@@ -138,7 +138,10 @@ def tile_mdlstm_t_v_kernel(
 
         def interleave(g, copy, w0, w1):
             if w1 > w0:
-                copy(out=st["dzoi", g][:, w0:w1, :], in_=st["dzo", g][:, :, w0:w1].rearrange("p j w -> p w j"))
+                copy(
+                    out=st["dzoi", g][:, w0:w1, :].rearrange("p (c i) j -> p c j i", i=4),
+                    in_=st["dzo", g][:, :, w0:w1].rearrange("p j (c i) -> p c j i", i=4),
+                )
 
         def quantize(nm, g, src, fmt, js=(0, 4)):
             if js[0] == 0:

@@ -232,149 +232,148 @@ def tile_mdlstm_t_v_kernel(
         s_copy = nc.scalar.copy
         v_copy = nc.vector.tensor_copy
 
-        with tc.manual_schedule():
-            nc.scalar.activation(out=warm[:], in_=neg_half[:], func=ACT.Tanh)
-            alloc_in(0)
-            for js in SLOTS:
-                load("c", c_v, 0, js)
-                load("g", g_v, 0, js)
-                load("o", o_v, 0, js)
-            alloc_in(1)
-            load("c", c_v, 1)
-            load("x", x_v, 0)
-            load_w("wo", wo)
-            load_w("wc", wc)
-            load("x", x_v, 1)
-            load("g", g_v, 1)
-            load("o", o_v, 1)
-            alloc_act(0)
-            for js in SLOTS:
-                act_th(0, js)
-                act_t2(0, js)
-                act_cq(0, js)
-            x_move(0)
+        nc.scalar.activation(out=warm[:], in_=neg_half[:], func=ACT.Tanh)
+        alloc_in(0)
+        for js in SLOTS:
+            load("c", c_v, 0, js)
+            load("g", g_v, 0, js)
+            load("o", o_v, 0, js)
+        alloc_in(1)
+        load("c", c_v, 1)
+        load("x", x_v, 0)
+        load_w("wo", wo)
+        load_w("wc", wc)
+        load("x", x_v, 1)
+        load("g", g_v, 1)
+        load("o", o_v, 1)
+        alloc_act(0)
+        for js in SLOTS:
+            act_th(0, js)
+            act_t2(0, js)
+            act_cq(0, js)
+        x_move(0)
 
-            for i in range(NCH):
-                nxt = i + 1 < NCH
-                last = i == NCH - 1
-                if i + 2 < NCH:
-                    load_chunk(i + 2)
-                alloc_v(i)
-                if nxt:
-                    alloc_act(i + 1)
-                if i == 0:
-                    for js in SLOTS:
-                        v_p(0, js)
-                        v_q(0, js)
-                        v_m(0, js)
-                        v_dzo(0, js)
-                        v_dzc(0, js)
-                    act_th(1)
-                    x_evac(0, (s_copy, s_copy))
-                    for nm in ("wo", "wc"):
-                        for js in HALVES:
-                            transposes(nm, 0, js)
-                    act_cq(1)
-                    for nm in ("wo", "wc"):
-                        for js in HALVES:
-                            copy_out(nm, 0, js, s_copy)
+        for i in range(NCH):
+            nxt = i + 1 < NCH
+            last = i == NCH - 1
+            if i + 2 < NCH:
+                load_chunk(i + 2)
+            alloc_v(i)
+            if nxt:
+                alloc_act(i + 1)
+            if i == 0:
+                for js in SLOTS:
+                    v_p(0, js)
+                    v_q(0, js)
+                    v_m(0, js)
+                    v_dzo(0, js)
+                    v_dzc(0, js)
+                act_th(1)
+                x_evac(0, (s_copy, s_copy))
+                for nm in ("wo", "wc"):
                     for js in HALVES:
-                        transposes("dzo", 0, js)
-                    x_move(1)
-                    act_t2(1)
-                    interleave(0, v_copy, 0, V_SHARE[0])
-                    quantize("woq", 0, st["wo_gr", 0], E4M3)
-                    quantize("wcq", 0, st["wc_gr", 0], E4M3)
-                    interleave(0, s_copy, V_SHARE[0], W)
+                        transposes(nm, 0, js)
+                act_cq(1)
+                for nm in ("wo", "wc"):
                     for js in HALVES:
-                        copy_out("dzo", 0, js, s_copy)
-                    quantize("xq", 0, st["xi", 0], E4M3)
-                    continue
+                        copy_out(nm, 0, js, s_copy)
                 for js in HALVES:
-                    transposes("dzc", i - 1, js)
-                v_p(i)
-                quantize("tokq", i - 1, st["dzoi", i - 1], E5M2)
-                out1(i - 1)
-                if nxt:
-                    act_th(i + 1)
-                x_evac(i, (s_copy, s_copy))
-                if nxt:
-                    act_cq(i + 1)
+                    transposes("dzo", 0, js)
+                x_move(1)
+                act_t2(1)
+                interleave(0, v_copy, 0, V_SHARE[0])
+                quantize("woq", 0, st["wo_gr", 0], E4M3)
+                quantize("wcq", 0, st["wc_gr", 0], E4M3)
+                interleave(0, s_copy, V_SHARE[0], W)
                 for js in HALVES:
-                    copy_out("dzc", i - 1, js, s_copy)
-                v_q(i)
-                quantize("oTq", i - 1, st["dzo_gr", i - 1], E5M2)
-                if last:
-                    quantize("cTq", i - 1, st["dzc_gr", i - 1], E5M2)
-                    v_dzo(i)
-                else:
-                    v_dzo(i)
-                    quantize("cTq", i - 1, st["dzc_gr", i - 1], E5M2)
-                for j in range(PACK):
-                    out0(i - 1, j)
-                if nxt:
-                    act_t2(i + 1)
-                evac(i - 1, 0, s_copy)
-                evac(i - 1, 1, s_copy)
-                store(i - 1, 0, 2)
+                    copy_out("dzo", 0, js, s_copy)
+                quantize("xq", 0, st["xi", 0], E4M3)
+                continue
+            for js in HALVES:
+                transposes("dzc", i - 1, js)
+            v_p(i)
+            quantize("tokq", i - 1, st["dzoi", i - 1], E5M2)
+            out1(i - 1)
+            if nxt:
+                act_th(i + 1)
+            x_evac(i, (s_copy, s_copy))
+            if nxt:
+                act_cq(i + 1)
+            for js in HALVES:
+                copy_out("dzc", i - 1, js, s_copy)
+            v_q(i)
+            quantize("oTq", i - 1, st["dzo_gr", i - 1], E5M2)
+            if last:
+                quantize("cTq", i - 1, st["dzc_gr", i - 1], E5M2)
+                v_dzo(i)
+            else:
+                v_dzo(i)
+                quantize("cTq", i - 1, st["dzc_gr", i - 1], E5M2)
+            for j in range(PACK):
+                out0(i - 1, j)
+            if nxt:
+                act_t2(i + 1)
+            evac(i - 1, 0, s_copy)
+            evac(i - 1, 1, s_copy)
+            store(i - 1, 0, 2)
+            for js in HALVES:
+                transposes("dzo", i, js)
+            if last:
+                interleave(i, s_copy, V_SHARE[i], W)
+                evac(i - 1, 2, s_copy)
+                evac(i - 1, 3, s_copy)
+                store(i - 1, 2, 4)
+            if not last:
+                v_m(i)
+                interleave(i, v_copy, 0, V_SHARE[i])
+                interleave(i, s_copy, V_SHARE[i], W)
+                evac(i - 1, 2, s_copy)
+                evac(i - 1, 3, s_copy)
+                store(i - 1, 2, 4)
+                x_move(i + 1)
                 for js in HALVES:
-                    transposes("dzo", i, js)
-                if last:
-                    interleave(i, s_copy, V_SHARE[i], W)
-                    evac(i - 1, 2, s_copy)
-                    evac(i - 1, 3, s_copy)
-                    store(i - 1, 2, 4)
-                if not last:
-                    v_m(i)
-                    interleave(i, v_copy, 0, V_SHARE[i])
-                    interleave(i, s_copy, V_SHARE[i], W)
-                    evac(i - 1, 2, s_copy)
-                    evac(i - 1, 3, s_copy)
-                    store(i - 1, 2, 4)
-                    x_move(i + 1)
-                    for js in HALVES:
-                        copy_out("dzo", i, js, s_copy)
-                    v_dzc(i)
-                    quantize("xq", i, st["xi", i], E4M3)
-                else:
-                    quantize("xq", i, st["xi", i], E4M3)
-                    interleave(i, v_copy, 0, V_SHARE[i])
-                    v_m(i, (0, 2))
-                    quantize("tokq", i, st["dzoi", i], E5M2)
-                    out1(i)
-                    for js in HALVES:
-                        copy_out("dzo", i, js, s_copy)
-                    v_dzc(i, (0, 2))
-                    transposes("dzc", i, (0, 2))
-                    dws = sb.tile([P, PACK, W], F32, name="dws", tag="dws")
-                    s_copy(out=dws[:, 0, :], in_=acc[0][:])
-                    s_copy(out=dws[:, 1, :], in_=acc[1][:])
-                    nc.sync.dma_start(out=dw_v[:, 0:2, :], in_=dws[:, 0:2, :])
-                    v_m(i, (2, 3))
-                    quantize("oTq", i, st["dzo_gr", i], E5M2)
-                    v_dzc(i, (2, 3))
-                    transposes("dzc", i, (2, 3))
-                    copy_out("dzc", i, (0, 2), s_copy)
-                    v_m(i, (3, 4))
-                    quantize("cTq", i, st["dzc_gr", i], E5M2, (0, 2))
-                    out0(i, 0)
-                    out0(i, 1)
-                    v_dzc(i, (3, 4))
-                    transposes("dzc", i, (3, 4))
-                    s_copy(out=dws[:, 2, :], in_=acc[2][:])
-                    copy_out("dzc", i, (2, 3), s_copy)
-                    quantize("cTq", i, st["dzc_gr", i], E5M2, (2, 3))
-                    out0(i, 2)
-                    s_copy(out=dws[:, 3, :], in_=acc[3][:])
-                    nc.sync.dma_start(out=dw_v[:, 2:4, :], in_=dws[:, 2:4, :])
-                    evac(i, 0, v_copy)
-                    store(i, 0, 1)
-                    copy_out("dzc", i, (3, 4), s_copy)
-                    quantize("cTq", i, st["dzc_gr", i], E5M2, (3, 4))
-                    out0(i, 3)
-                    evac(i, 1, s_copy)
-                    store(i, 1, 2)
-                    evac(i, 2, v_copy)
-                    store(i, 2, 3)
-                    evac(i, 3, s_copy)
-                    store(i, 3, 4)
+                    copy_out("dzo", i, js, s_copy)
+                v_dzc(i)
+                quantize("xq", i, st["xi", i], E4M3)
+            else:
+                quantize("xq", i, st["xi", i], E4M3)
+                interleave(i, v_copy, 0, V_SHARE[i])
+                v_m(i, (0, 2))
+                quantize("tokq", i, st["dzoi", i], E5M2)
+                out1(i)
+                for js in HALVES:
+                    copy_out("dzo", i, js, s_copy)
+                v_dzc(i, (0, 2))
+                transposes("dzc", i, (0, 2))
+                dws = sb.tile([P, PACK, W], F32, name="dws", tag="dws")
+                s_copy(out=dws[:, 0, :], in_=acc[0][:])
+                s_copy(out=dws[:, 1, :], in_=acc[1][:])
+                nc.sync.dma_start(out=dw_v[:, 0:2, :], in_=dws[:, 0:2, :])
+                v_m(i, (2, 3))
+                quantize("oTq", i, st["dzo_gr", i], E5M2)
+                v_dzc(i, (2, 3))
+                transposes("dzc", i, (2, 3))
+                copy_out("dzc", i, (0, 2), s_copy)
+                v_m(i, (3, 4))
+                quantize("cTq", i, st["dzc_gr", i], E5M2, (0, 2))
+                out0(i, 0)
+                out0(i, 1)
+                v_dzc(i, (3, 4))
+                transposes("dzc", i, (3, 4))
+                s_copy(out=dws[:, 2, :], in_=acc[2][:])
+                copy_out("dzc", i, (2, 3), s_copy)
+                quantize("cTq", i, st["dzc_gr", i], E5M2, (2, 3))
+                out0(i, 2)
+                s_copy(out=dws[:, 3, :], in_=acc[3][:])
+                nc.sync.dma_start(out=dw_v[:, 2:4, :], in_=dws[:, 2:4, :])
+                evac(i, 0, v_copy)
+                store(i, 0, 1)
+                copy_out("dzc", i, (3, 4), s_copy)
+                quantize("cTq", i, st["dzc_gr", i], E5M2, (3, 4))
+                out0(i, 3)
+                evac(i, 1, s_copy)
+                store(i, 1, 2)
+                evac(i, 2, v_copy)
+                store(i, 2, 3)
+                evac(i, 3, s_copy)
+                store(i, 3, 4)

from contextlib import ExitStack

import concourse.mybir as mybir
from concourse.masks import make_identity

T, N, K = 4096, 512, 512
FLOPS = 3 * 2 * T * N * K
BYTES = 2 * T * K + 2 * 2 * K * N + 2 * 4 * T * N + 2 * T * N + 4 * T * K + 4 * K * N

F32 = mybir.dt.float32
BF16 = mybir.dt.bfloat16
U32 = mybir.dt.uint32
U8 = mybir.dt.uint8
E4M3 = mybir.dt.float8_e4m3fn_x4
E5M2 = mybir.dt.float8_e5m2_x4
ACT = mybir.ActivationFunctionType
ALU = mybir.AluOpType

P = 128
PACK = 4
W = 512
CHUNK = P * PACK
NCH = T // CHUNK

V_SHARE = (512, 256, 192, 192, 192, 192, 192, 128)
HALVES = ((0, 2), (2, 4))
SLOTS = ((0, 1), (1, 2), (2, 3), (3, 4))


def tile_mdlstm_t_v_kernel(
    tc, x, wf, uf, biasf, wi, ui, biasi, wo, uo, biaso, wc, uc, biasc, o, c, grad_out, out_0, out_1
):
    nc = tc.nc

    def chunks(ap):
        return ap.flatten_outer_dims().rearrange("(g p j) w -> g p j w", p=P, j=PACK)

    x_v = chunks(x)
    o_v = chunks(o)
    c_v = chunks(c)
    g_v = chunks(grad_out)
    dx_v = chunks(out_0)
    dw_v = out_1.rearrange("(a p) n -> p a n", p=P)

    def flat(t, js=(0, 4)):
        return t[:, js[0] : js[1], :].rearrange("p j w -> p (j w)")

    with ExitStack() as ctx:
        sb = ctx.enter_context(tc.tile_pool(name="sb", bufs=1))
        ps = ctx.enter_context(tc.psum_pool(name="ps", bufs=1))

        ident = sb.tile([P, P], F32, name="ident", tag="ident")
        make_identity(nc, ident[:])
        ident_bf = sb.tile([P, P], BF16, name="ident_bf", tag="ident_bf")
        make_identity(nc, ident_bf[:])
        neg_half = sb.tile([P, 1], F32, name="neg_half", tag="neg_half")
        nc.vector.memset(neg_half[:], -0.5)
        warm = sb.tile([P, 1], F32, name="warm", tag="warm")

        acc = []
        for a in range(4):
            acc_a = ps.tile([P, W], F32, name="acc%d" % a, tag="acc%d" % a)
            acc.append(acc_a)

        st = {}

        def alloc_in(g):
            for nm, dt_, nb in (("c", F32, 3), ("o", F32, 3), ("g", BF16, 3), ("x", BF16, 2)):
                t = sb.tile([P, PACK, W], dt_, name=nm, tag=nm, bufs=nb)
                st[nm, g] = t

        def load(nm, view, g, js=(0, 4)):
            nc.sync.dma_start(out=st[nm, g][:, js[0] : js[1], :], in_=view[g][:, js[0] : js[1], :])

        def load_chunk(g):
            alloc_in(g)
            load("c", c_v, g)
            load("x", x_v, g)
            load("g", g_v, g)
            load("o", o_v, g)

        def load_w(nm, w_ap):
            t = sb.tile([P, PACK, W], BF16, name=nm, tag=nm)
            nc.sync.dma_start(out=t[:], in_=w_ap.rearrange("(a p) n -> p a n", p=P))
            st[nm, 0] = t

        def alloc_act(g):
            th = sb.tile([P, PACK, W], F32, name="th", tag="th", bufs=2)
            t2 = sb.tile([P, PACK, W], F32, name="t2", tag="t2", bufs=2)
            st["th", g] = th
            st["t2", g] = t2

        def act_th(g, js=(0, 4)):
            nc.scalar.activation(out=flat(st["th", g], js), in_=flat(st["c", g], js), func=ACT.Tanh)

        def act_cq(g, js=(0, 4)):
            nc.scalar.activation(out=flat(st["c", g], js), in_=flat(st["c", g], js), func=ACT.Square, bias=neg_half[:, 0:1])

        def act_t2(g, js=(0, 4)):
            nc.scalar.activation(out=flat(st["t2", g], js), in_=flat(st["th", g], js), func=ACT.Square)

        def alloc_v(g):
            pt = sb.tile([P, PACK, W], F32, name="pt", tag="pt")
            dzo = sb.tile([P, PACK, W], BF16, name="dzo", tag="dzo", bufs=2)
            dzc = sb.tile([P, PACK, W], BF16, name="dzc", tag="dzc", bufs=2)
            dzoi = sb.tile([P, W, PACK], BF16, name="dzoi", tag="dzoi", bufs=2, align_bytes=64)
            st["pt", g] = pt
            st["dzo", g] = dzo
            st["dzc", g] = dzc
            st["dzoi", g] = dzoi

        def v_p(g, js=(0, 4)):
            nc.vector.tensor_tensor(out=flat(st["pt", g], js), in0=flat(st["g", g], js), in1=flat(st["o", g], js), op=ALU.mult)

        def v_q(g, js=(0, 4)):
            nc.vector.scalar_tensor_tensor(
                out=flat(st["o", g], js), in0=flat(st["o", g], js), scalar=1.0, in1=flat(st["th", g], js),
                op0=ALU.subtract, op1=ALU.mult,
            )

        def v_dzo(g, js=(0, 4)):
            nc.vector.scalar_tensor_tensor(
                out=flat(st["dzo", g], js), in0=flat(st["pt", g], js), scalar=-1.0, in1=flat(st["o", g], js),
                op0=ALU.mult, op1=ALU.mult,
            )

        def v_m(g, js=(0, 4)):
            nc.vector.scalar_tensor_tensor(
                out=flat(st["t2", g], js), in0=flat(st["t2", g], js), scalar=1.0, in1=flat(st["pt", g], js),
                op0=ALU.subtract, op1=ALU.mult,
            )

        def v_dzc(g, js=(0, 4)):
            nc.vector.scalar_tensor_tensor(
                out=flat(st["dzc", g], js), in0=flat(st["c", g], js), scalar=0.25, in1=flat(st["t2", g], js),
                op0=ALU.subtract, op1=ALU.mult,
            )

        def interleave(g, copy, w0, w1):
            if w1 > w0:
                copy(
                    out=st["dzoi", g][:, w0:w1, :].rearrange("p (c i) j -> p c j i", i=4),
                    in_=st["dzo", g][:, :, w0:w1].rearrange("p j (c i) -> p c j i", i=4),
                )

        def quantize(nm, g, src, fmt, js=(0, 4)):
            if js[0] == 0:
                codes = sb.tile([P, W], U32, name=nm + "_c", tag=nm + "_c", align_bytes=64)
                scales = sb.tile([P, W], U8, name=nm + "_s", tag=nm + "_s", align_bytes=64)
                st[nm, g] = (codes, scales)
            codes, scales = st[nm, g]
            cols = slice(js[0] * P, js[1] * P)
            if src.ndim == 4:
                part = src[:, js[0] : js[1], :, :].rearrange("p a b c -> p (a b c)")
            else:
                part = src[:].rearrange("p a b -> p (a b)")
            nc.vector.quantize_mx(out=codes[:, cols].bitcast(fmt), scales=scales[:, cols], in_=part)

        def bank():
            b = ps.tile([P, W], F32, name="bank", tag="bank", bufs=4)
            return b

        def transposes(nm, g, js):
            n = js[1] - js[0]
            tp = bank()
            tv = tp[:, 0 : n * 2 * P].rearrange("m (a u p) -> m a u p", a=n, u=2)
            for a in range(n):
                words = flat(st[nm, g], (js[0] + a, js[0] + a + 1)).bitcast(F32)
                for u in range(2):
                    nc.tensor.transpose(tv[:, a, u, :], words[:, u : W // 2 : 2], ident[:])
            st[nm + "_tp", g, js[0]] = tp

        def copy_out(nm, g, js, copy):
            n = js[1] - js[0]
            if js[0] == 0:
                grouped = sb.tile([P, PACK, P, PACK], BF16, name=nm + "_gr", tag=nm + "_gr", align_bytes=64)
                st[nm + "_gr", g] = grouped
            dst = st[nm + "_gr", g][:].bitcast(F32)
            tp = st[nm + "_tp", g, js[0]]
            copy(out=dst[:, js[0] : js[1], :, :], in_=tp[:, 0 : n * 2 * P].rearrange("m (a u p) -> m a p u", a=n, u=2))

        def x_move(g):
            for h in range(2):
                xb = bank()
                xb_bf = xb[:].bitcast(BF16)
                for r in range(2):
                    w0 = (2 * h + r) * P
                    nc.tensor.matmul(
                        out=xb_bf[:, r * W : (r + 1) * W], lhsT=ident_bf[:],
                        rhs=st["x", g][:, :, w0 : w0 + P].rearrange("p j w -> p w j"), start=True, stop=True,
                    )
                st["xb", g, h] = xb

        def x_evac(g, copies):
            xi = sb.tile([P, 2, 2 * W], BF16, name="xi", tag="xi", bufs=2, align_bytes=64)
            for h in range(2):
                cp = copies[h]
                cp(out=xi[:, h, :], in_=st["xb", g, h][:].bitcast(BF16))
            st["xi", g] = xi

        def out1(g):
            xc, xs = st["xq", g]
            dc, ds = st["tokq", g]
            for a in range(4):
                cols = slice(a * P, (a + 1) * P)
                nc.tensor.matmul_mx(
                    out=acc[a][:], lhsT=xc[:, cols].bitcast(E4M3), lhsT_scale=xs[:, cols],
                    rhs=dc[:].bitcast(E5M2), rhs_scale=ds[:], start=(g == 0), stop=(g == NCH - 1),
                )

        def out0(g, j):
            op = bank()
            cols = slice(j * P, (j + 1) * P)
            for idx, (dn, wn) in enumerate((("oTq", "woq"), ("cTq", "wcq"))):
                dc, ds = st[dn, g]
                wcod, wsc = st[wn, 0]
                nc.tensor.matmul_mx(
                    out=op[:], lhsT=dc[:, cols].bitcast(E5M2), lhsT_scale=ds[:, cols],
                    rhs=wcod[:].bitcast(E4M3), rhs_scale=wsc[:], start=(idx == 0), stop=(idx == 1),
                )
            st["op", g, j] = op

        def evac(g, j, copy):
            if j == 0:
                dxs = sb.tile([P, PACK, W], F32, name="dxs", tag="dxs", bufs=2)
                st["dxs", g] = dxs
            copy(out=st["dxs", g][:, j, :], in_=st["op", g, j][:])

        def store(g, j0, j1):
            nc.sync.dma_start(out=dx_v[g][:, j0:j1, :], in_=st["dxs", g][:, j0:j1, :])

        s_copy = nc.scalar.copy
        v_copy = nc.vector.tensor_copy

        nc.scalar.activation(out=warm[:], in_=neg_half[:], func=ACT.Tanh)
        alloc_in(0)
        for js in SLOTS:
            load("c", c_v, 0, js)
            load("g", g_v, 0, js)
            load("o", o_v, 0, js)
        alloc_in(1)
        load("c", c_v, 1)
        load("x", x_v, 0)
        load_w("wo", wo)
        load_w("wc", wc)
        load("x", x_v, 1)
        load("g", g_v, 1)
        load("o", o_v, 1)
        alloc_act(0)
        for js in SLOTS:
            act_th(0, js)
            act_t2(0, js)
            act_cq(0, js)
        x_move(0)

        for i in range(NCH):
            nxt = i + 1 < NCH
            last = i == NCH - 1
            if i + 2 < NCH:
                load_chunk(i + 2)
            alloc_v(i)
            if nxt:
                alloc_act(i + 1)
            if i == 0:
                for js in SLOTS:
                    v_p(0, js)
                    v_q(0, js)
                    v_m(0, js)
                    v_dzo(0, js)
                    v_dzc(0, js)
                act_th(1)
                x_evac(0, (s_copy, s_copy))
                for nm in ("wo", "wc"):
                    for js in HALVES:
                        transposes(nm, 0, js)
                act_cq(1)
                for nm in ("wo", "wc"):
                    for js in HALVES:
                        copy_out(nm, 0, js, s_copy)
                for js in HALVES:
                    transposes("dzo", 0, js)
                x_move(1)
                act_t2(1)
                interleave(0, v_copy, 0, V_SHARE[0])
                quantize("woq", 0, st["wo_gr", 0], E4M3)
                quantize("wcq", 0, st["wc_gr", 0], E4M3)
                interleave(0, s_copy, V_SHARE[0], W)
                for js in HALVES:
                    copy_out("dzo", 0, js, s_copy)
                quantize("xq", 0, st["xi", 0], E4M3)
                continue
            for js in HALVES:
                transposes("dzc", i - 1, js)
            v_p(i)
            quantize("tokq", i - 1, st["dzoi", i - 1], E5M2)
            out1(i - 1)
            if nxt:
                act_th(i + 1)
            x_evac(i, (s_copy, s_copy))
            if nxt:
                act_cq(i + 1)
            for js in HALVES:
                copy_out("dzc", i - 1, js, s_copy)
            v_q(i)
            quantize("oTq", i - 1, st["dzo_gr", i - 1], E5M2)
            if last:
                quantize("cTq", i - 1, st["dzc_gr", i - 1], E5M2)
                v_dzo(i)
            else:
                v_dzo(i)
                quantize("cTq", i - 1, st["dzc_gr", i - 1], E5M2)
            for j in range(PACK):
                out0(i - 1, j)
            if nxt:
                act_t2(i + 1)
            evac(i - 1, 0, s_copy)
            evac(i - 1, 1, s_copy)
            store(i - 1, 0, 2)
            for js in HALVES:
                transposes("dzo", i, js)
            if last:
                interleave(i, s_copy, V_SHARE[i], W)
                evac(i - 1, 2, s_copy)
                evac(i - 1, 3, s_copy)
                store(i - 1, 2, 4)
            if not last:
                v_m(i)
                interleave(i, v_copy, 0, V_SHARE[i])
                interleave(i, s_copy, V_SHARE[i], W)
                evac(i - 1, 2, s_copy)
                evac(i - 1, 3, s_copy)
                store(i - 1, 2, 4)
                x_move(i + 1)
                for js in HALVES:
                    copy_out("dzo", i, js, s_copy)
                v_dzc(i)
                quantize("xq", i, st["xi", i], E4M3)
            else:
                quantize("xq", i, st["xi", i], E4M3)
                interleave(i, v_copy, 0, V_SHARE[i])
                v_m(i, (0, 2))
                quantize("tokq", i, st["dzoi", i], E5M2)
                out1(i)
                for js in HALVES:
                    copy_out("dzo", i, js, s_copy)
                v_dzc(i, (0, 2))
                transposes("dzc", i, (0, 2))
                dws = sb.tile([P, PACK, W], F32, name="dws", tag="dws")
                s_copy(out=dws[:, 0, :], in_=acc[0][:])
                s_copy(out=dws[:, 1, :], in_=acc[1][:])
                nc.sync.dma_start(out=dw_v[:, 0:2, :], in_=dws[:, 0:2, :])
                v_m(i, (2, 3))
                quantize("oTq", i, st["dzo_gr", i], E5M2)
                v_dzc(i, (2, 3))
                transposes("dzc", i, (2, 3))
                copy_out("dzc", i, (0, 2), s_copy)
                v_m(i, (3, 4))
                quantize("cTq", i, st["dzc_gr", i], E5M2, (0, 2))
                out0(i, 0)
                out0(i, 1)
                v_dzc(i, (3, 4))
                transposes("dzc", i, (3, 4))
                s_copy(out=dws[:, 2, :], in_=acc[2][:])
                copy_out("dzc", i, (2, 3), s_copy)
                quantize("cTq", i, st["dzc_gr", i], E5M2, (2, 3))
                out0(i, 2)
                s_copy(out=dws[:, 3, :], in_=acc[3][:])
                nc.sync.dma_start(out=dw_v[:, 2:4, :], in_=dws[:, 2:4, :])
                evac(i, 0, v_copy)
                store(i, 0, 1)
                copy_out("dzc", i, (3, 4), s_copy)
                quantize("cTq", i, st["dzc_gr", i], E5M2, (3, 4))
                out0(i, 3)
                evac(i, 1, s_copy)
                store(i, 1, 2)
                evac(i, 2, v_copy)
                store(i, 2, 3)
                evac(i, 3, s_copy)
                store(i, 3, 4)
